import numpy as np
import ml_dtypes


def mxq(x, axis, fmt="e4m3"):
    dtype, down = {"e4m3": (ml_dtypes.float8_e4m3fn, 7), "e5m2": (ml_dtypes.float8_e5m2, 14)}[fmt]
    v = np.moveaxis(np.asarray(x, np.float32).astype(ml_dtypes.bfloat16).astype(np.float64), axis, -1)
    blocks = v.reshape(v.shape[:-1] + (-1, 32))
    amax = np.abs(blocks).max(-1, keepdims=True)
    byte = np.maximum(np.where(amax > 0, np.frexp(amax)[1] - 1 + 127, 0) - down, 1)
    scale = np.exp2(byte - 127.0)
    codes = (blocks / scale).astype(np.float32).astype(dtype).astype(np.float64)
    return np.moveaxis((codes * scale).reshape(v.shape), -1, axis)


WIDE = False


def mx_kscale(k):
    if not WIDE:
        return np.ones(k)
    levels = np.array([10, -10, 5, -5, 0])
    a = np.random.permutation(np.resize(levels, k // 512 * 4)).reshape(k // 512, 4)
    idx = np.arange(k)
    return np.exp2(a[idx // 512, idx % 128 // 32])


BF16 = ml_dtypes.bfloat16


def bf(x):
    return np.asarray(x, np.float32).astype(BF16)


def f64(x):
    return np.asarray(x).astype(np.float64)


B, S, D, R = 2, 1024, 1024, 8
EPS = 1e-6


def setup_inputs():
    s, t = mx_kscale(D), mx_kscale(D)
    return {"x": bf(np.random.standard_normal((B, S, D)) * s),
            "pos_emb": bf(np.random.standard_normal((1, S, D)) * s),
            "enc_w0": bf(np.random.standard_normal((D, D)) / np.sqrt(D) / s[None, :] * t[:, None]),
            "enc_w1": bf(np.random.standard_normal((D, D)) / np.sqrt(D) / t[None, :])}


def reference(x, pos_emb, enc_w0, enc_w1):
    x = f64(x)
    y = x + f64(pos_emb)[:, : x.shape[1]]
    h = np.maximum(mxq(y, 2, "e4m3") @ mxq(f64(enc_w0), 1, "e4m3").T, 0.0)
    h = np.maximum(mxq(h, 2, "e4m3") @ mxq(f64(enc_w1), 1, "e4m3").T, 0.0)
    return h / (np.sqrt((h * h).sum(-1, keepdims=True)) + EPS)

@@ -1,0 +1,242 @@
+from contextlib import ExitStack
+
+import concourse.mybir as mybir
+from concourse.masks import make_identity
+
+BF16 = mybir.dt.bfloat16
+F32 = mybir.dt.float32
+U32 = mybir.dt.uint32
+U8 = mybir.dt.uint8
+FP8X4 = mybir.dt.float8_e4m3fn_x4
+ACT = mybir.ActivationFunctionType
+ALU = mybir.AluOpType
+
+P = 128
+D = 1024
+TOKENS = 2048
+POSITIONS = 1024
+PACK = 4
+PASSES = D // (P * PACK)
+WORD_TILES = D // 2 // P
+PAIR = 2
+ROUND = PAIR * P
+ROUNDS = TOKENS // ROUND
+POS_ROUNDS = POSITIONS // ROUND
+HALF = 512
+HALVES = D // HALF
+EPS = 1e-6
+
+FLOPS = 2 * 2 * TOKENS * D * D
+
+
+def tile_mybadtransfomerblock_pa_kernel(tc, x, pos_emb, enc_w0, enc_w1, out):
+    nc = tc.nc
+
+    x_rounds = x.flatten_outer_dims().rearrange("(r p i) d -> r p i d", p=P, i=PAIR)
+    pos_rounds = pos_emb.flatten_outer_dims().rearrange("(r p i) d -> r p i d", p=P, i=PAIR)
+    out_rounds = out.flatten_outer_dims().rearrange("(r p i) d -> r p i d", p=P, i=PAIR)
+    w0_pairs = enc_w0.rearrange("(a p e) k -> a p e k", p=P, e=PAIR)
+    w1_pairs = enc_w1.rearrange("(a e p) k -> a p e k", p=P, e=PAIR)
+
+    with ExitStack() as ctx:
+        const = ctx.enter_context(tc.tile_pool(name="const", bufs=1))
+        raw = ctx.enter_context(tc.tile_pool(name="raw", bufs=1))
+        keep = ctx.enter_context(tc.tile_pool(name="keep", bufs=1))
+        two = ctx.enter_context(tc.tile_pool(name="two", bufs=2))
+        three = ctx.enter_context(tc.tile_pool(name="three", bufs=3))
+        psum = ctx.enter_context(tc.psum_pool(name="psum", bufs=8))
+
+        warm = const.tile([P, 1], F32)
+        nc.vector.memset(warm[:], 1.0)
+        nc.scalar.sqrt(warm[:], warm[:])
+
+        ident = const.tile([P, P], F32)
+        make_identity(nc, ident[:])
+
+        def load(name, source):
+            rows = raw.tile([P, PAIR, D], BF16, name=name)
+            nc.sync.dma_start(out=rows[:], in_=source)
+            return rows
+
+        x_sb = {}
+        pos_sb = {}
+        x_sb[0] = load("x_sb0", x_rounds[0])
+        pos_sb[0] = load("pos_sb0", pos_rounds[0])
+        w0_sb = [load("w0_sb%d" % a, w0_pairs[a]) for a in range(D // ROUND)]
+        x_sb[1] = load("x_sb1", x_rounds[1])
+        pos_sb[1] = load("pos_sb1", pos_rounds[1])
+        w1_sb = [load("w1_sb%d" % a, w1_pairs[a]) for a in range(D // ROUND)]
+        for r in range(2, ROUNDS):
+            x_sb[r] = load("x_sb%d" % r, x_rounds[r])
+            if r < POS_ROUNDS:
+                pos_sb[r] = load("pos_sb%d" % r, pos_rounds[r])
+
+        def transpose_rows(rows, copy_out, grouped_words):
+            bank = psum.tile([P, WORD_TILES, P], F32, tag="bank")
+            words = rows.bitcast(F32)
+            for c in range(WORD_TILES):
+                nc.tensor.transpose(bank[:, c, :], words[:, c * P : (c + 1) * P], ident[:])
+            copy_out(out=grouped_words, in_=bank[:].rearrange("p (g u) c -> p g c u", u=2))
+
+        def quantise(grouped, codes, scales):
+            nc.vector.quantize_mx(
+                out=codes[:].rearrange("p g c -> p (g c)").bitcast(FP8X4),
+                scales=scales[:].rearrange("p g c -> p (g c)"),
+                in_=grouped[:].rearrange("p g c t -> p (g c t)"),
+            )
+
+        def prepare_weight(name, pairs):
+            codes = []
+            scales = []
+            for h in range(HALVES):
+                w_grouped = two.tile([P, PASSES, HALF, PACK], BF16, align_bytes=64)
+                w_words = w_grouped[:].bitcast(F32)
+                for j in range(HALF // P):
+                    copy_out = nc.scalar.copy if j % 2 == 0 else nc.vector.tensor_copy
+                    transpose_rows(
+                        pairs[(HALF // ROUND) * h + j // PAIR][:, j % PAIR, :],
+                        copy_out,
+                        w_words[:, :, j * P : (j + 1) * P, :],
+                    )
+                w_codes = keep.tile(
+                    [P, PASSES, HALF], U32, name="%s_codes%d" % (name, h), align_bytes=64
+                )
+                w_scales = keep.tile(
+                    [P, PASSES, HALF], U8, name="%s_scales%d" % (name, h), align_bytes=64
+                )
+                quantise(w_grouped, w_codes, w_scales)
+                codes.append(w_codes)
+                scales.append(w_scales)
+            return codes, scales
+
+        pos_grouped = {}
+        y_grouped = {}
+        y_codes = {}
+        y_scales = {}
+        h1_grouped = {}
+        h1_codes = {}
+        h1_scales = {}
+        h2 = {}
+        norm = {}
+
+        def make_y(r):
+            x_g = two.tile([P, PASSES, ROUND, PACK], BF16, name="x_g")
+            for i in range(PAIR):
+                transpose_rows(
+                    x_sb[r][:, i, :],
+                    nc.scalar.copy,
+                    x_g[:].bitcast(F32)[:, :, i * P : (i + 1) * P, :],
+                )
+            if r < POS_ROUNDS:
+                pos_g = keep.tile([P, PASSES, ROUND, PACK], BF16, name="pos_g%d" % r)
+                for i in range(PAIR):
+                    transpose_rows(
+                        pos_sb[r][:, i, :],
+                        nc.vector.tensor_copy,
+                        pos_g[:].bitcast(F32)[:, :, i * P : (i + 1) * P, :],
+                    )
+                pos_grouped[r] = pos_g
+            y_g = two.tile([P, PASSES, ROUND, PACK], BF16, name="y_g", align_bytes=64)
+            nc.vector.tensor_tensor(
+                out=y_g[:].rearrange("p g c t -> p (g c t)"),
+                in0=x_g[:].rearrange("p g c t -> p (g c t)"),
+                in1=pos_grouped[r % POS_ROUNDS][:].rearrange("p g c t -> p (g c t)"),
+                op=ALU.add,
+            )
+            y_grouped[r] = y_g
+
+        def quantise_y(r):
+            y_c = three.tile([P, PASSES, ROUND], U32, name="y_c", align_bytes=64)
+            y_s = three.tile([P, PASSES, ROUND], U8, name="y_s", align_bytes=64)
+            quantise(y_grouped[r], y_c, y_s)
+            y_codes[r] = y_c
+            y_scales[r] = y_s
+
+        def layer_one(r):
+            h1_g = two.tile([P, PASSES, ROUND, PACK], BF16, name="h1_g", align_bytes=64)
+            for q in range(HALVES):
+                for i in range(PAIR):
+                    bank = psum.tile([P, PACK, P], F32, tag="bank")
+                    for t in range(PACK):
+                        for g in range(PASSES):
+                            nc.tensor.matmul_mx(
+                                out=bank[:, t, :],
+                                lhsT=w0_codes[q][:, g, t * P : (t + 1) * P].bitcast(FP8X4),
+                                lhsT_scale=w0_scales[q][:, g, t * P : (t + 1) * P],
+                                rhs=y_codes[r][:, g, i * P : (i + 1) * P].bitcast(FP8X4),
+                                rhs_scale=y_scales[r][:, g, i * P : (i + 1) * P],
+                                start=(g == 0),
+                                stop=(g == PASSES - 1),
+                            )
+                    nc.vector.tensor_scalar_max(
+                        out=h1_g[:, q, i * P : (i + 1) * P, :],
+                        in0=bank[:].rearrange("p t c -> p c t"),
+                        scalar1=0.0,
+                    )
+            h1_grouped[r] = h1_g
+
+        def quantise_h1(r):
+            h1_c = three.tile([P, PASSES, ROUND], U32, name="h1_c", align_bytes=64)
+            h1_s = three.tile([P, PASSES, ROUND], U8, name="h1_s", align_bytes=64)
+            quantise(h1_grouped[r], h1_c, h1_s)
+            h1_codes[r] = h1_c
+            h1_scales[r] = h1_s
+
+        def layer_two(r):
+            h2_r = three.tile([P, PAIR, D], F32, name="h2_r")
+            sum_sq = three.tile([P, PAIR], F32, name="sum_sq")
+            for i in range(PAIR):
+                for n in range(HALVES):
+                    bank = psum.tile([P, HALF], F32, tag="bank")
+                    for g in range(PASSES):
+                        nc.tensor.matmul_mx(
+                            out=bank[:],
+                            lhsT=h1_codes[r][:, g, i * P : (i + 1) * P].bitcast(FP8X4),
+                            lhsT_scale=h1_scales[r][:, g, i * P : (i + 1) * P],
+                            rhs=w1_codes[n][:, g, :].bitcast(FP8X4),
+                            rhs_scale=w1_scales[n][:, g, :],
+                            start=(g == 0),
+                            stop=(g == PASSES - 1),
+                        )
+                    nc.scalar.activation(
+                        out=h2_r[:, i, n * HALF : (n + 1) * HALF], in_=bank[:], func=ACT.Relu
+                    )
+                squares = two.tile([P, D], BF16, name="squares")
+                nc.scalar.activation(
+                    out=squares[:],
+                    in_=h2_r[:, i, :],
+                    func=ACT.Square,
+                    accum_out=sum_sq[:, i : i + 1],
+                )
+            norm_r = three.tile([P, PAIR], F32, name="norm_r")
+            nc.scalar.sqrt(norm_r[:], sum_sq[:])
+            h2[r] = h2_r
+            norm[r] = norm_r
+
+        def normalise(r):
+            inverse = three.tile([P, PAIR], F32, name="inverse")
+            nc.vector.tensor_scalar_add(out=inverse[:], in0=norm[r][:], scalar1=EPS)
+            nc.vector.reciprocal(out=inverse[:], in_=inverse[:])
+            for i in range(PAIR):
+                nc.vector.tensor_scalar_mul(
+                    out=h2[r][:, i, :], in0=h2[r][:, i, :], scalar1=inverse[:, i : i + 1]
+                )
+                nc.sync.dma_start(out=out_rounds[r][:, i, :], in_=h2[r][:, i, :])
+
+        for s in range(ROUNDS + 3):
+            if s < ROUNDS:
+                make_y(s)
+            if s == 0:
+                w0_codes, w0_scales = prepare_weight("w0", w0_sb)
+            if 1 <= s <= ROUNDS:
+                layer_one(s - 1)
+            if s == 1:
+                w1_codes, w1_scales = prepare_weight("w1", w1_sb)
+            if 3 <= s:
+                normalise(s - 3)
+            if s < ROUNDS:
+                quantise_y(s)
+            if 1 <= s <= ROUNDS:
+                quantise_h1(s - 1)
+            if 2 <= s <= ROUNDS + 1:
+                layer_two(s - 2)

@@ -44,7 +44,9 @@ def tile_mybadtransfomerblock_pa_kernel(tc, x, pos_emb, enc_w0, enc_w1, out):
         keep = ctx.enter_context(tc.tile_pool(name="keep", bufs=1))
         two = ctx.enter_context(tc.tile_pool(name="two", bufs=2))
         three = ctx.enter_context(tc.tile_pool(name="three", bufs=3))
+        four = ctx.enter_context(tc.tile_pool(name="four", bufs=4))
         psum = ctx.enter_context(tc.psum_pool(name="psum", bufs=8))
+        ctx.enter_context(tc.manual_schedule())
 
         warm = const.tile([P, 1], F32)
         nc.vector.memset(warm[:], 1.0)
@@ -168,10 +170,10 @@ def tile_mybadtransfomerblock_pa_kernel(tc, x, pos_emb, enc_w0, enc_w1, out):
                                 start=(g == 0),
                                 stop=(g == PASSES - 1),
                             )
-                    nc.vector.tensor_scalar_max(
+                    nc.scalar.activation(
                         out=h1_g[:, q, i * P : (i + 1) * P, :],
-                        in0=bank[:].rearrange("p t c -> p c t"),
-                        scalar1=0.0,
+                        in_=bank[:].rearrange("p t c -> p c t"),
+                        func=ACT.Relu,
                     )
             h1_grouped[r] = h1_g
 
@@ -183,8 +185,7 @@ def tile_mybadtransfomerblock_pa_kernel(tc, x, pos_emb, enc_w0, enc_w1, out):
             h1_scales[r] = h1_s
 
         def layer_two(r):
-            h2_r = three.tile([P, PAIR, D], F32, name="h2_r")
-            sum_sq = three.tile([P, PAIR], F32, name="sum_sq")
+            h2_r = four.tile([P, PAIR, D], F32, name="h2_r")
             for i in range(PAIR):
                 for n in range(HALVES):
                     bank = psum.tile([P, HALF], F32, tag="bank")
@@ -198,45 +199,55 @@ def tile_mybadtransfomerblock_pa_kernel(tc, x, pos_emb, enc_w0, enc_w1, out):
                             start=(g == 0),
                             stop=(g == PASSES - 1),
                         )
-                    nc.scalar.activation(
-                        out=h2_r[:, i, n * HALF : (n + 1) * HALF], in_=bank[:], func=ACT.Relu
+                    nc.vector.tensor_scalar_max(
+                        out=h2_r[:, i, n * HALF : (n + 1) * HALF], in0=bank[:], scalar1=0.0
                     )
+            h2[r] = h2_r
+
+        def take_norm(r):
+            sum_sq = four.tile([P, PAIR], F32, name="sum_sq")
+            for i in range(PAIR):
                 squares = two.tile([P, D], BF16, name="squares")
                 nc.scalar.activation(
                     out=squares[:],
-                    in_=h2_r[:, i, :],
+                    in_=h2[r][:, i, :],
                     func=ACT.Square,
                     accum_out=sum_sq[:, i : i + 1],
                 )
-            norm_r = three.tile([P, PAIR], F32, name="norm_r")
+            norm_r = four.tile([P, PAIR], F32, name="norm_r")
             nc.scalar.sqrt(norm_r[:], sum_sq[:])
-            h2[r] = h2_r
             norm[r] = norm_r
 
         def normalise(r):
-            inverse = three.tile([P, PAIR], F32, name="inverse")
+            inverse = four.tile([P, PAIR], F32, name="inverse")
             nc.vector.tensor_scalar_add(out=inverse[:], in0=norm[r][:], scalar1=EPS)
             nc.vector.reciprocal(out=inverse[:], in_=inverse[:])
             for i in range(PAIR):
-                nc.vector.tensor_scalar_mul(
-                    out=h2[r][:, i, :], in0=h2[r][:, i, :], scalar1=inverse[:, i : i + 1]
+                nc.gpsimd.tensor_scalar(
+                    out=h2[r][:, i, :],
+                    in0=h2[r][:, i, :],
+                    scalar1=inverse[:, i : i + 1],
+                    scalar2=0.0,
+                    op0=ALU.mult,
+                    op1=ALU.add,
                 )
                 nc.sync.dma_start(out=out_rounds[r][:, i, :], in_=h2[r][:, i, :])
 
-        for s in range(ROUNDS + 3):
+        for s in range(ROUNDS + 4):
             if s < ROUNDS:
                 make_y(s)
+                quantise_y(s)
             if s == 0:
                 w0_codes, w0_scales = prepare_weight("w0", w0_sb)
             if 1 <= s <= ROUNDS:
                 layer_one(s - 1)
+            if 0 <= s - 3 < ROUNDS:
+                take_norm(s - 3)
             if s == 1:
                 w1_codes, w1_scales = prepare_weight("w1", w1_sb)
-            if 3 <= s:
-                normalise(s - 3)
-            if s < ROUNDS:
-                quantise_y(s)
             if 1 <= s <= ROUNDS:
                 quantise_h1(s - 1)
-            if 2 <= s <= ROUNDS + 1:
+            if 0 <= s - 4 < ROUNDS:
+                normalise(s - 4)
+            if 0 <= s - 2 < ROUNDS:
                 layer_two(s - 2)

@@ -111,7 +111,9 @@ def tile_mybadtransfomerblock_pa_kernel(tc, x, pos_emb, enc_w0, enc_w1, out):
                 scales.append(w_scales)
             return codes, scales
 
+        x_grouped = {}
         pos_grouped = {}
+        sum_squares = {}
         y_grouped = {}
         y_codes = {}
         y_scales = {}
@@ -121,27 +123,30 @@ def tile_mybadtransfomerblock_pa_kernel(tc, x, pos_emb, enc_w0, enc_w1, out):
         h2 = {}
         norm = {}
 
-        def make_y(r):
+        def transpose_inputs(r):
             x_g = two.tile([P, PASSES, ROUND, PACK], BF16, name="x_g")
             for i in range(PAIR):
                 transpose_rows(
                     x_sb[r][:, i, :],
-                    nc.scalar.copy,
+                    nc.scalar.copy if i == 0 else nc.vector.tensor_copy,
                     x_g[:].bitcast(F32)[:, :, i * P : (i + 1) * P, :],
                 )
+            x_grouped[r] = x_g
             if r < POS_ROUNDS:
                 pos_g = keep.tile([P, PASSES, ROUND, PACK], BF16, name="pos_g%d" % r)
                 for i in range(PAIR):
                     transpose_rows(
                         pos_sb[r][:, i, :],
-                        nc.vector.tensor_copy,
+                        nc.scalar.copy,
                         pos_g[:].bitcast(F32)[:, :, i * P : (i + 1) * P, :],
                     )
                 pos_grouped[r] = pos_g
+
+        def add_positions(r):
             y_g = two.tile([P, PASSES, ROUND, PACK], BF16, name="y_g", align_bytes=64)
             nc.vector.tensor_tensor(
                 out=y_g[:].rearrange("p g c t -> p (g c t)"),
-                in0=x_g[:].rearrange("p g c t -> p (g c t)"),
+                in0=x_grouped[r][:].rearrange("p g c t -> p (g c t)"),
                 in1=pos_grouped[r % POS_ROUNDS][:].rearrange("p g c t -> p (g c t)"),
                 op=ALU.add,
             )
@@ -204,26 +209,30 @@ def tile_mybadtransfomerblock_pa_kernel(tc, x, pos_emb, enc_w0, enc_w1, out):
                     )
             h2[r] = h2_r
 
-        def take_norm(r):
-            sum_sq = four.tile([P, PAIR], F32, name="sum_sq")
-            for i in range(PAIR):
-                squares = two.tile([P, D], BF16, name="squares")
-                nc.scalar.activation(
-                    out=squares[:],
-                    in_=h2[r][:, i, :],
-                    func=ACT.Square,
-                    accum_out=sum_sq[:, i : i + 1],
-                )
+        def square(r, i):
+            if i == 0:
+                sum_sq = four.tile([P, PAIR], F32, name="sum_sq")
+                sum_squares[r] = sum_sq
+            squares = two.tile([P, D], BF16, name="squares")
+            nc.scalar.activation(
+                out=squares[:],
+                in_=h2[r][:, i, :],
+                func=ACT.Square,
+                accum_out=sum_squares[r][:, i : i + 1],
+            )
+
+        def take_root(r):
             norm_r = four.tile([P, PAIR], F32, name="norm_r")
-            nc.scalar.sqrt(norm_r[:], sum_sq[:])
+            nc.scalar.sqrt(norm_r[:], sum_squares[r][:])
             norm[r] = norm_r
 
         def normalise(r):
             inverse = four.tile([P, PAIR], F32, name="inverse")
             nc.vector.tensor_scalar_add(out=inverse[:], in0=norm[r][:], scalar1=EPS)
             nc.vector.reciprocal(out=inverse[:], in_=inverse[:])
+            scaler = nc.vector if r == ROUNDS - 1 else nc.gpsimd
             for i in range(PAIR):
-                nc.gpsimd.tensor_scalar(
+                scaler.tensor_scalar(
                     out=h2[r][:, i, :],
                     in0=h2[r][:, i, :],
                     scalar1=inverse[:, i : i + 1],
@@ -235,19 +244,24 @@ def tile_mybadtransfomerblock_pa_kernel(tc, x, pos_emb, enc_w0, enc_w1, out):
 
         for s in range(ROUNDS + 4):
             if s < ROUNDS:
-                make_y(s)
+                transpose_inputs(s)
+            if 0 <= s - 2 < ROUNDS:
+                quantise_h1(s - 2)
+            if s < ROUNDS:
+                add_positions(s)
+            if 0 <= s - 4:
+                normalise(s - 4)
+            if s < ROUNDS:
                 quantise_y(s)
             if s == 0:
                 w0_codes, w0_scales = prepare_weight("w0", w0_sb)
-            if 1 <= s <= ROUNDS:
+            if 0 <= s - 1 < ROUNDS:
                 layer_one(s - 1)
             if 0 <= s - 3 < ROUNDS:
-                take_norm(s - 3)
+                square(s - 3, 0)
+                square(s - 3, 1)
+                take_root(s - 3)
             if s == 1:
                 w1_codes, w1_scales = prepare_weight("w1", w1_sb)
-            if 1 <= s <= ROUNDS:
-                quantise_h1(s - 1)
-            if 0 <= s - 4 < ROUNDS:
-                normalise(s - 4)
             if 0 <= s - 2 < ROUNDS:
                 layer_two(s - 2)

from contextlib import ExitStack

import concourse.mybir as mybir
from concourse.masks import make_identity

BF16 = mybir.dt.bfloat16
F32 = mybir.dt.float32
U32 = mybir.dt.uint32
U8 = mybir.dt.uint8
FP8X4 = mybir.dt.float8_e4m3fn_x4
ACT = mybir.ActivationFunctionType
ALU = mybir.AluOpType

P = 128
D = 1024
TOKENS = 2048
POSITIONS = 1024
PACK = 4
PASSES = D // (P * PACK)
WORD_TILES = D // 2 // P
PAIR = 2
ROUND = PAIR * P
ROUNDS = TOKENS // ROUND
POS_ROUNDS = POSITIONS // ROUND
HALF = 512
HALVES = D // HALF
EPS = 1e-6

FLOPS = 2 * 2 * TOKENS * D * D


def tile_mybadtransfomerblock_pa_kernel(tc, x, pos_emb, enc_w0, enc_w1, out):
    nc = tc.nc

    x_rounds = x.flatten_outer_dims().rearrange("(r p i) d -> r p i d", p=P, i=PAIR)
    pos_rounds = pos_emb.flatten_outer_dims().rearrange("(r p i) d -> r p i d", p=P, i=PAIR)
    out_rounds = out.flatten_outer_dims().rearrange("(r p i) d -> r p i d", p=P, i=PAIR)
    w0_pairs = enc_w0.rearrange("(a p e) k -> a p e k", p=P, e=PAIR)
    w1_pairs = enc_w1.rearrange("(a e p) k -> a p e k", p=P, e=PAIR)

    with ExitStack() as ctx:
        const = ctx.enter_context(tc.tile_pool(name="const", bufs=1))
        raw = ctx.enter_context(tc.tile_pool(name="raw", bufs=1))
        keep = ctx.enter_context(tc.tile_pool(name="keep", bufs=1))
        two = ctx.enter_context(tc.tile_pool(name="two", bufs=2))
        three = ctx.enter_context(tc.tile_pool(name="three", bufs=3))
        four = ctx.enter_context(tc.tile_pool(name="four", bufs=4))
        psum = ctx.enter_context(tc.psum_pool(name="psum", bufs=8))
        ctx.enter_context(tc.manual_schedule())

        warm = const.tile([P, 1], F32)
        nc.vector.memset(warm[:], 1.0)
        nc.scalar.sqrt(warm[:], warm[:])

        ident = const.tile([P, P], F32)
        make_identity(nc, ident[:])

        def load(name, source):
            rows = raw.tile([P, PAIR, D], BF16, name=name)
            nc.sync.dma_start(out=rows[:], in_=source)
            return rows

        x_sb = {}
        pos_sb = {}
        x_sb[0] = load("x_sb0", x_rounds[0])
        pos_sb[0] = load("pos_sb0", pos_rounds[0])
        w0_sb = [load("w0_sb%d" % a, w0_pairs[a]) for a in range(D // ROUND)]
        x_sb[1] = load("x_sb1", x_rounds[1])
        pos_sb[1] = load("pos_sb1", pos_rounds[1])
        w1_sb = [load("w1_sb%d" % a, w1_pairs[a]) for a in range(D // ROUND)]
        for r in range(2, ROUNDS):
            x_sb[r] = load("x_sb%d" % r, x_rounds[r])
            if r < POS_ROUNDS:
                pos_sb[r] = load("pos_sb%d" % r, pos_rounds[r])

        def transpose_rows(rows, copy_out, grouped_words):
            bank = psum.tile([P, WORD_TILES, P], F32, tag="bank")
            words = rows.bitcast(F32)
            for c in range(WORD_TILES):
                nc.tensor.transpose(bank[:, c, :], words[:, c * P : (c + 1) * P], ident[:])
            copy_out(out=grouped_words, in_=bank[:].rearrange("p (g u) c -> p g c u", u=2))

        def quantise(grouped, codes, scales):
            nc.vector.quantize_mx(
                out=codes[:].rearrange("p g c -> p (g c)").bitcast(FP8X4),
                scales=scales[:].rearrange("p g c -> p (g c)"),
                in_=grouped[:].rearrange("p g c t -> p (g c t)"),
            )

        def prepare_weight(name, pairs):
            codes = []
            scales = []
            for h in range(HALVES):
                w_grouped = two.tile([P, PASSES, HALF, PACK], BF16, align_bytes=64)
                w_words = w_grouped[:].bitcast(F32)
                for j in range(HALF // P):
                    copy_out = nc.scalar.copy if j % 2 == 0 else nc.vector.tensor_copy
                    transpose_rows(
                        pairs[(HALF // ROUND) * h + j // PAIR][:, j % PAIR, :],
                        copy_out,
                        w_words[:, :, j * P : (j + 1) * P, :],
                    )
                w_codes = keep.tile(
                    [P, PASSES, HALF], U32, name="%s_codes%d" % (name, h), align_bytes=64
                )
                w_scales = keep.tile(
                    [P, PASSES, HALF], U8, name="%s_scales%d" % (name, h), align_bytes=64
                )
                quantise(w_grouped, w_codes, w_scales)
                codes.append(w_codes)
                scales.append(w_scales)
            return codes, scales

        x_grouped = {}
        pos_grouped = {}
        sum_squares = {}
        y_grouped = {}
        y_codes = {}
        y_scales = {}
        h1_grouped = {}
        h1_codes = {}
        h1_scales = {}
        h2 = {}
        norm = {}

        def transpose_inputs(r):
            x_g = two.tile([P, PASSES, ROUND, PACK], BF16, name="x_g")
            for i in range(PAIR):
                transpose_rows(
                    x_sb[r][:, i, :],
                    nc.scalar.copy if i == 0 else nc.vector.tensor_copy,
                    x_g[:].bitcast(F32)[:, :, i * P : (i + 1) * P, :],
                )
            x_grouped[r] = x_g
            if r < POS_ROUNDS:
                pos_g = keep.tile([P, PASSES, ROUND, PACK], BF16, name="pos_g%d" % r)
                for i in range(PAIR):
                    transpose_rows(
                        pos_sb[r][:, i, :],
                        nc.scalar.copy,
                        pos_g[:].bitcast(F32)[:, :, i * P : (i + 1) * P, :],
                    )
                pos_grouped[r] = pos_g

        def add_positions(r):
            y_g = two.tile([P, PASSES, ROUND, PACK], BF16, name="y_g", align_bytes=64)
            nc.vector.tensor_tensor(
                out=y_g[:].rearrange("p g c t -> p (g c t)"),
                in0=x_grouped[r][:].rearrange("p g c t -> p (g c t)"),
                in1=pos_grouped[r % POS_ROUNDS][:].rearrange("p g c t -> p (g c t)"),
                op=ALU.add,
            )
            y_grouped[r] = y_g

        def quantise_y(r):
            y_c = three.tile([P, PASSES, ROUND], U32, name="y_c", align_bytes=64)
            y_s = three.tile([P, PASSES, ROUND], U8, name="y_s", align_bytes=64)
            quantise(y_grouped[r], y_c, y_s)
            y_codes[r] = y_c
            y_scales[r] = y_s

        def layer_one(r):
            h1_g = two.tile([P, PASSES, ROUND, PACK], BF16, name="h1_g", align_bytes=64)
            for q in range(HALVES):
                for i in range(PAIR):
                    bank = psum.tile([P, PACK, P], F32, tag="bank")
                    for t in range(PACK):
                        for g in range(PASSES):
                            nc.tensor.matmul_mx(
                                out=bank[:, t, :],
                                lhsT=w0_codes[q][:, g, t * P : (t + 1) * P].bitcast(FP8X4),
                                lhsT_scale=w0_scales[q][:, g, t * P : (t + 1) * P],
                                rhs=y_codes[r][:, g, i * P : (i + 1) * P].bitcast(FP8X4),
                                rhs_scale=y_scales[r][:, g, i * P : (i + 1) * P],
                                start=(g == 0),
                                stop=(g == PASSES - 1),
                            )
                    nc.scalar.activation(
                        out=h1_g[:, q, i * P : (i + 1) * P, :],
                        in_=bank[:].rearrange("p t c -> p c t"),
                        func=ACT.Relu,
                    )
            h1_grouped[r] = h1_g

        def quantise_h1(r):
            h1_c = three.tile([P, PASSES, ROUND], U32, name="h1_c", align_bytes=64)
            h1_s = three.tile([P, PASSES, ROUND], U8, name="h1_s", align_bytes=64)
            quantise(h1_grouped[r], h1_c, h1_s)
            h1_codes[r] = h1_c
            h1_scales[r] = h1_s

        def layer_two(r):
            h2_r = four.tile([P, PAIR, D], F32, name="h2_r")
            for i in range(PAIR):
                for n in range(HALVES):
                    bank = psum.tile([P, HALF], F32, tag="bank")
                    for g in range(PASSES):
                        nc.tensor.matmul_mx(
                            out=bank[:],
                            lhsT=h1_codes[r][:, g, i * P : (i + 1) * P].bitcast(FP8X4),
                            lhsT_scale=h1_scales[r][:, g, i * P : (i + 1) * P],
                            rhs=w1_codes[n][:, g, :].bitcast(FP8X4),
                            rhs_scale=w1_scales[n][:, g, :],
                            start=(g == 0),
                            stop=(g == PASSES - 1),
                        )
                    nc.vector.tensor_scalar_max(
                        out=h2_r[:, i, n * HALF : (n + 1) * HALF], in0=bank[:], scalar1=0.0
                    )
            h2[r] = h2_r

        def square(r, i):
            if i == 0:
                sum_sq = four.tile([P, PAIR], F32, name="sum_sq")
                sum_squares[r] = sum_sq
            squares = two.tile([P, D], BF16, name="squares")
            nc.scalar.activation(
                out=squares[:],
                in_=h2[r][:, i, :],
                func=ACT.Square,
                accum_out=sum_squares[r][:, i : i + 1],
            )

        def take_root(r):
            norm_r = four.tile([P, PAIR], F32, name="norm_r")
            nc.scalar.sqrt(norm_r[:], sum_squares[r][:])
            norm[r] = norm_r

        def normalise(r):
            inverse = four.tile([P, PAIR], F32, name="inverse")
            nc.vector.tensor_scalar_add(out=inverse[:], in0=norm[r][:], scalar1=EPS)
            nc.vector.reciprocal(out=inverse[:], in_=inverse[:])
            scaler = nc.vector if r == ROUNDS - 1 else nc.gpsimd
            for i in range(PAIR):
                scaler.tensor_scalar(
                    out=h2[r][:, i, :],
                    in0=h2[r][:, i, :],
                    scalar1=inverse[:, i : i + 1],
                    scalar2=0.0,
                    op0=ALU.mult,
                    op1=ALU.add,
                )
                nc.sync.dma_start(out=out_rounds[r][:, i, :], in_=h2[r][:, i, :])

        for s in range(ROUNDS + 4):
            if s < ROUNDS:
                transpose_inputs(s)
            if 0 <= s - 2 < ROUNDS:
                quantise_h1(s - 2)
            if s < ROUNDS:
                add_positions(s)
            if 0 <= s - 4:
                normalise(s - 4)
            if s < ROUNDS:
                quantise_y(s)
            if s == 0:
                w0_codes, w0_scales = prepare_weight("w0", w0_sb)
            if 0 <= s - 1 < ROUNDS:
                layer_one(s - 1)
            if 0 <= s - 3 < ROUNDS:
                square(s - 3, 0)
                square(s - 3, 1)
                take_root(s - 3)
            if s == 1:
                w1_codes, w1_scales = prepare_weight("w1", w1_sb)
            if 0 <= s - 2 < ROUNDS:
                layer_two(s - 2)
